import numpy as np
import ml_dtypes


def mxq(x, axis, fmt="e4m3"):
    dtype, down = {"e4m3": (ml_dtypes.float8_e4m3fn, 7), "e5m2": (ml_dtypes.float8_e5m2, 14)}[fmt]
    v = np.moveaxis(np.asarray(x, np.float32).astype(ml_dtypes.bfloat16).astype(np.float64), axis, -1)
    blocks = v.reshape(v.shape[:-1] + (-1, 32))
    amax = np.abs(blocks).max(-1, keepdims=True)
    byte = np.maximum(np.where(amax > 0, np.frexp(amax)[1] - 1 + 127, 0) - down, 1)
    scale = np.exp2(byte - 127.0)
    codes = (blocks / scale).astype(np.float32).astype(dtype).astype(np.float64)
    return np.moveaxis((codes * scale).reshape(v.shape), -1, axis)


WIDE = False


def mx_kscale(k):
    if not WIDE:
        return np.ones(k)
    levels = np.array([10, -10, 5, -5, 0])
    if k % 512:
        return np.exp2(np.random.permutation(np.resize(levels, k // 32))).repeat(32)
    a = np.empty((k // 512, 16))
    for p in range(k // 512):
        a[p, :8] = np.random.permutation(np.resize(levels, 8))
        for g in range(8):
            far = levels[np.abs(levels - a[p, g]) >= 10]
            a[p, g + 8] = far[np.random.randint(len(far))]
    return np.exp2(a.ravel()).repeat(32)


BF16 = ml_dtypes.bfloat16


def bf(x):
    return np.asarray(x, np.float32).astype(BF16)


def f64(x):
    return np.asarray(x).astype(np.float64)


B, M, F, U = 4096, 4, 512, 256


def setup_inputs():
    s = mx_kscale(F)
    limit = np.sqrt(6.0 / (F + U))
    return {"x": bf(np.random.standard_normal((B, M, F)) * s),
            "W": bf(np.random.uniform(-limit, limit, (M, F, U)) / s[None, :, None]),
            "b": bf(np.random.standard_normal((M, U)) * 0.1)}


def reference(x, W, b):
    xq = mxq(f64(x), 2, "e4m3")
    wq = mxq(f64(W), 1, "e4m3")
    y = (xq.transpose(1, 0, 2) @ wq).transpose(1, 0, 2)
    y = np.maximum(y + f64(b)[None, :, :], 0.0)
    return y.reshape(y.shape[0], -1)

@@ -1,0 +1,223 @@
+from contextlib import ExitStack
+
+import concourse.mybir as mybir
+from concourse.masks import make_identity
+
+F32 = mybir.dt.float32
+BF16 = mybir.dt.bfloat16
+U32 = mybir.dt.uint32
+U8 = mybir.dt.uint8
+FP8X4 = mybir.dt.float8_e4m3fn_x4
+ADD = mybir.AluOpType.add
+RELU = mybir.ActivationFunctionType.Relu
+
+P = 128
+ROWS, MASKS, FEAT, UNITS = 4096, 4, 512, 256
+FLOPS = 2 * ROWS * MASKS * FEAT * UNITS
+
+NT = ROWS // P
+T = 4
+G = NT // T
+XW = MASKS * FEAT
+OW = MASKS * UNITS
+DEPTH = 4
+PIN = True
+
+LOAD_UNITS = [(0, 1), (1, 1), (2, 2), (4, 2), (6, 2)] + [(T * g, T) for g in range(2, G)]
+N_HEAD = 5 + (DEPTH - 2)
+STORE_UNITS = [(2 * j, 2) for j in range(NT // 2 - 1)] + [(NT - 2, 1), (NT - 1, 1)]
+
+
+def tile_paralleldense_t_kernel(tc, x, W, b, out):
+    nc = tc.nc
+    x_v = x.rearrange("(g p t) m f -> g p (t m f)", g=G, p=P, t=T)
+    out_v = out.rearrange("(g p t) n -> g p (t n)", g=G, p=P, t=T)
+    w_v = W.rearrange("m (q t) c -> q m (t c)", q=P, t=4)
+
+    with ExitStack() as ctx:
+        if PIN:
+            ctx.enter_context(tc.manual_schedule())
+        const = ctx.enter_context(tc.tile_pool(name="const", bufs=1))
+        xpool = ctx.enter_context(tc.tile_pool(name="xpool", bufs=DEPTH))
+        opool = ctx.enter_context(tc.tile_pool(name="opool", bufs=6))
+        gpool = ctx.enter_context(tc.tile_pool(name="gpool", bufs=3))
+        qpool = ctx.enter_context(tc.tile_pool(name="qpool", bufs=3))
+        tpool = ctx.enter_context(tc.psum_pool(name="tpool", bufs=4))
+        apool = ctx.enter_context(tc.psum_pool(name="apool", bufs=4))
+
+        x_words = {}
+
+        def load(unit):
+            i0, n = LOAD_UNITS[unit]
+            g, t0 = divmod(i0, T)
+            if n == T:
+                x_sb = xpool.tile([P, n * XW], BF16, name="x_sb")
+            else:
+                x_sb = const.tile([P, n * XW], BF16, name="x_head%d" % unit)
+            nc.sync.dma_start(out=x_sb[:], in_=x_v[g][:, t0 * XW : (t0 + n) * XW])
+            words = x_sb[:].bitcast(F32)
+            for k in range(n):
+                x_words[i0 + k] = (words, k * (XW // 2))
+
+        ident = const.tile([P, P], F32, name="ident")
+        make_identity(nc, ident[:])
+        load(0)
+        brow = const.tile([P, OW], BF16, name="brow")
+        nc.vector.memset(brow[:], 0.0)
+        nc.sync.dma_start(out=brow[0:1, :], in_=b.rearrange("(o m) u -> o (m u)", o=1))
+        ones = const.tile([P, P], BF16, name="ones")
+        nc.vector.memset(ones[:], 1.0)
+        w_raw = const.tile([P, MASKS, 4, UNITS], BF16, name="w_raw")
+        for m0 in (0, 2):
+            nc.sync.dma_start(
+                out=w_raw[:, m0 : m0 + 2].rearrange("q m t c -> q m (t c)"),
+                in_=w_v[:, m0 : m0 + 2],
+            )
+        for unit in range(1, N_HEAD):
+            load(unit)
+
+        bias = const.tile([P, OW], F32, name="bias")
+        bias_banks = []
+
+        def bias_matmuls():
+            for h in range(2):
+                bp = apool.tile([P, 512], F32, name="acc")
+                nc.tensor.matmul(out=bp[:], lhsT=ones[:], rhs=brow[:, 512 * h : 512 * h + 512], start=True, stop=True)
+                bias_banks.append(bp)
+
+        def bias_copies():
+            for h in range(2):
+                nc.scalar.copy(out=bias[:, 512 * h : 512 * h + 512], in_=bias_banks[h][:])
+
+        w_grp = const.tile([P, MASKS, UNITS, 4], BF16, name="w_grp", align_bytes=64)
+        w_codes = const.tile([P, MASKS * UNITS], U32, name="w_codes", align_bytes=64)
+        w_scales = const.tile([P, MASKS * UNITS], U8, name="w_scales", align_bytes=64)
+
+        def w_regroup(m):
+            nc.vector.tensor_copy(
+                out=w_grp[:, m].rearrange("q (c i) t -> q c t i", i=4),
+                in_=w_raw[:, m].rearrange("q t (c i) -> q c t i", i=4),
+            )
+
+        def w_quantise(m):
+            cols = slice(UNITS * m, UNITS * m + UNITS)
+            nc.vector.quantize_mx(
+                out=w_codes[:, cols].bitcast(FP8X4),
+                scales=w_scales[:, cols],
+                in_=w_grp[:, m].rearrange("q c t -> q (c t)"),
+            )
+
+        tp_of, grp_of, q_of, acc_of, o_of = {}, {}, {}, {}, {}
+
+        def transposes(i):
+            words, c0 = x_words[i]
+            banks = []
+            for h in range(2):
+                tpb = tpool.tile([P, 512], F32, name="tpb")
+                for j in range(4):
+                    ml, u = divmod(j, 2)
+                    col = c0 + 256 * (2 * h + ml) + u
+                    nc.tensor.transpose(tpb[:, P * j : P * j + P], words[:, col : col + 255 : 2], ident[:])
+                banks.append(tpb)
+            tp_of[i] = banks
+
+        def copies(i):
+            grp = gpool.tile([P, 4 * MASKS * P], BF16, name="grp", align_bytes=64)
+            gw = grp[:].bitcast(F32)
+            for h in range(2):
+                nc.scalar.copy(
+                    out=gw[:, 512 * h : 512 * h + 512].rearrange("q (m i u) -> q m i u", m=2, u=2),
+                    in_=tp_of[i][h][:].rearrange("q (m u i) -> q m i u", m=2, u=2),
+                )
+            grp_of[i] = grp
+
+        def quantise(i):
+            codes = qpool.tile([P, MASKS * P], U32, name="codes", align_bytes=64)
+            scales = qpool.tile([P, MASKS * P], U8, name="scales", align_bytes=64)
+            nc.vector.quantize_mx(out=codes[:].bitcast(FP8X4), scales=scales[:], in_=grp_of[i][:])
+            q_of[i] = (codes, scales)
+
+        def passes(i):
+            codes, scales = q_of[i]
+            banks = []
+            for h in range(2):
+                acc = apool.tile([P, 512], F32, name="acc")
+                for ml in range(2):
+                    m = 2 * h + ml
+                    nc.tensor.matmul_mx(
+                        out=acc[:, UNITS * ml : UNITS * ml + UNITS],
+                        lhsT=codes[:, P * m : P * m + P].bitcast(FP8X4),
+                        lhsT_scale=scales[:, P * m : P * m + P],
+                        rhs=w_codes[:, UNITS * m : UNITS * m + UNITS].bitcast(FP8X4),
+                        rhs_scale=w_scales[:, UNITS * m : UNITS * m + UNITS],
+                        start=True,
+                        stop=True,
+                    )
+                banks.append(acc)
+            acc_of[i] = banks
+
+        unit_of = {}
+        for j, (i0, n) in enumerate(STORE_UNITS):
+            for k in range(n):
+                unit_of[i0 + k] = j
+
+        def adds(i):
+            j = unit_of[i]
+            i0, n = STORE_UNITS[j]
+            if i == i0:
+                o_of[j] = opool.tile([P, n * OW], F32, name="o_sb")
+            o_sb = o_of[j]
+            c0 = (i - i0) * OW
+            for h in range(2):
+                nc.vector.tensor_tensor(
+                    out=o_sb[:, c0 + 512 * h : c0 + 512 * h + 512],
+                    in0=acc_of[i][h][:],
+                    in1=bias[:, 512 * h : 512 * h + 512],
+                    op=ADD,
+                )
+
+        def relu_store(i):
+            j = unit_of[i]
+            i0, n = STORE_UNITS[j]
+            o_sb = o_of[j]
+            c0 = (i - i0) * OW
+            lo = o_sb[:, c0 : c0 + 512]
+            hi = o_sb[:, c0 + 512 : c0 + OW]
+            nc.scalar.activation(out=lo, in_=lo, func=RELU)
+            if (i % 2 == 1 and i < NT - 4) or i == NT - 1:
+                nc.vector.tensor_scalar_max(out=hi, in0=hi, scalar1=0.0)
+            else:
+                nc.scalar.activation(out=hi, in_=hi, func=RELU)
+            if i == i0 + n - 1:
+                g, t0 = divmod(i0, T)
+                nc.sync.dma_start(out=out_v[g][:, t0 * OW : (t0 + n) * OW], in_=o_sb[:])
+            if i % T == T - 1:
+                unit = N_HEAD + i // T
+                if unit < len(LOAD_UNITS):
+                    load(unit)
+
+        transposes(0)
+        bias_matmuls()
+        w_regroup(0)
+        w_regroup(1)
+        w_quantise(0)
+        w_quantise(1)
+        w_regroup(2)
+        w_regroup(3)
+        w_quantise(2)
+        w_quantise(3)
+        for s in range(NT + 3):
+            if s + 1 < NT:
+                transposes(s + 1)
+            if 0 <= s - 1 < NT:
+                quantise(s - 1)
+            if s < NT:
+                copies(s)
+            if s == 0:
+                bias_copies()
+            if 0 <= s - 1 < NT:
+                passes(s - 1)
+            if 0 <= s - 2 < NT:
+                adds(s - 2)
+            if 0 <= s - 3 < NT:
+                relu_store(s - 3)

@@ -16,64 +16,57 @@ ROWS, MASKS, FEAT, UNITS = 4096, 4, 512, 256
 FLOPS = 2 * ROWS * MASKS * FEAT * UNITS
 
 NT = ROWS // P
-T = 4
-G = NT // T
 XW = MASKS * FEAT
 OW = MASKS * UNITS
-DEPTH = 4
 PIN = True
+V_RELU = 512
 
-LOAD_UNITS = [(0, 1), (1, 1), (2, 2), (4, 2), (6, 2)] + [(T * g, T) for g in range(2, G)]
-N_HEAD = 5 + (DEPTH - 2)
-STORE_UNITS = [(2 * j, 2) for j in range(NT // 2 - 1)] + [(NT - 2, 1), (NT - 1, 1)]
+LOAD_UNITS = [(0, 1), (1, 1), (2, 1), (3, 1), (4, 2), (6, 2), (8, 4), (12, 4), (16, 8), (24, 8)]
+STORE_UNITS = [(0, 8), (8, 8), (16, 4), (20, 4), (24, 2), (26, 2), (28, 1), (29, 1), (30, 1), (31, 1)]
 
 
 def tile_paralleldense_t_kernel(tc, x, W, b, out):
     nc = tc.nc
-    x_v = x.rearrange("(g p t) m f -> g p (t m f)", g=G, p=P, t=T)
-    out_v = out.rearrange("(g p t) n -> g p (t n)", g=G, p=P, t=T)
+    x_v = x.rearrange("(p t) m f -> p (t m f)", p=P, t=NT)
+    out_v = out.rearrange("(p t) n -> p (t n)", p=P, t=NT)
     w_v = W.rearrange("m (q t) c -> q m (t c)", q=P, t=4)
 
     with ExitStack() as ctx:
         if PIN:
             ctx.enter_context(tc.manual_schedule())
         const = ctx.enter_context(tc.tile_pool(name="const", bufs=1))
-        xpool = ctx.enter_context(tc.tile_pool(name="xpool", bufs=DEPTH))
-        opool = ctx.enter_context(tc.tile_pool(name="opool", bufs=6))
         gpool = ctx.enter_context(tc.tile_pool(name="gpool", bufs=3))
         qpool = ctx.enter_context(tc.tile_pool(name="qpool", bufs=3))
         tpool = ctx.enter_context(tc.psum_pool(name="tpool", bufs=4))
         apool = ctx.enter_context(tc.psum_pool(name="apool", bufs=4))
 
-        x_words = {}
+        xo = const.tile([P, NT * XW], BF16, name="xo")
+        words = xo[:].bitcast(F32)
 
         def load(unit):
             i0, n = LOAD_UNITS[unit]
-            g, t0 = divmod(i0, T)
-            if n == T:
-                x_sb = xpool.tile([P, n * XW], BF16, name="x_sb")
-            else:
-                x_sb = const.tile([P, n * XW], BF16, name="x_head%d" % unit)
-            nc.sync.dma_start(out=x_sb[:], in_=x_v[g][:, t0 * XW : (t0 + n) * XW])
-            words = x_sb[:].bitcast(F32)
-            for k in range(n):
-                x_words[i0 + k] = (words, k * (XW // 2))
+            cols = slice(i0 * XW, (i0 + n) * XW)
+            nc.sync.dma_start(out=xo[:, cols], in_=x_v[:, cols])
 
-        ident = const.tile([P, P], F32, name="ident")
-        make_identity(nc, ident[:])
-        load(0)
         brow = const.tile([P, OW], BF16, name="brow")
-        nc.vector.memset(brow[:], 0.0)
-        nc.sync.dma_start(out=brow[0:1, :], in_=b.rearrange("(o m) u -> o (m u)", o=1))
+        nc.vector.memset(brow[:].bitcast(U32), 0)
         ones = const.tile([P, P], BF16, name="ones")
         nc.vector.memset(ones[:], 1.0)
+        ident = const.tile([P, P], F32, name="ident")
+        make_identity(nc, ident[:])
         w_raw = const.tile([P, MASKS, 4, UNITS], BF16, name="w_raw")
-        for m0 in (0, 2):
+
+        def load_w(m0):
             nc.sync.dma_start(
                 out=w_raw[:, m0 : m0 + 2].rearrange("q m t c -> q m (t c)"),
                 in_=w_v[:, m0 : m0 + 2],
             )
-        for unit in range(1, N_HEAD):
+
+        load_w(0)
+        nc.sync.dma_start(out=brow[0:1, :], in_=b.rearrange("(o m) u -> o (m u)", o=1))
+        load(0)
+        load_w(2)
+        for unit in range(1, len(LOAD_UNITS)):
             load(unit)
 
         bias = const.tile([P, OW], F32, name="bias")
@@ -107,10 +100,10 @@ def tile_paralleldense_t_kernel(tc, x, W, b, out):
                 in_=w_grp[:, m].rearrange("q c t -> q (c t)"),
             )
 
-        tp_of, grp_of, q_of, acc_of, o_of = {}, {}, {}, {}, {}
+        tp_of, grp_of, q_of, acc_of = {}, {}, {}, {}
 
         def transposes(i):
-            words, c0 = x_words[i]
+            c0 = i * OW
             banks = []
             for h in range(2):
                 tpb = tpool.tile([P, 512], F32, name="tpb")
@@ -156,67 +149,54 @@ def tile_paralleldense_t_kernel(tc, x, W, b, out):
                 banks.append(acc)
             acc_of[i] = banks
 
-        unit_of = {}
-        for j, (i0, n) in enumerate(STORE_UNITS):
-            for k in range(n):
-                unit_of[i0 + k] = j
+        store_ending = {i0 + n - 1: (i0, n) for i0, n in STORE_UNITS}
 
         def adds(i):
-            j = unit_of[i]
-            i0, n = STORE_UNITS[j]
-            if i == i0:
-                o_of[j] = opool.tile([P, n * OW], F32, name="o_sb")
-            o_sb = o_of[j]
-            c0 = (i - i0) * OW
+            c0 = i * OW
             for h in range(2):
                 nc.vector.tensor_tensor(
-                    out=o_sb[:, c0 + 512 * h : c0 + 512 * h + 512],
+                    out=words[:, c0 + 512 * h : c0 + 512 * h + 512],
                     in0=acc_of[i][h][:],
                     in1=bias[:, 512 * h : 512 * h + 512],
                     op=ADD,
                 )
 
         def relu_store(i):
-            j = unit_of[i]
-            i0, n = STORE_UNITS[j]
-            o_sb = o_of[j]
-            c0 = (i - i0) * OW
-            lo = o_sb[:, c0 : c0 + 512]
-            hi = o_sb[:, c0 + 512 : c0 + OW]
-            nc.scalar.activation(out=lo, in_=lo, func=RELU)
-            if (i % 2 == 1 and i < NT - 4) or i == NT - 1:
-                nc.vector.tensor_scalar_max(out=hi, in0=hi, scalar1=0.0)
-            else:
-                nc.scalar.activation(out=hi, in_=hi, func=RELU)
-            if i == i0 + n - 1:
-                g, t0 = divmod(i0, T)
-                nc.sync.dma_start(out=out_v[g][:, t0 * OW : (t0 + n) * OW], in_=o_sb[:])
-            if i % T == T - 1:
-                unit = N_HEAD + i // T
-                if unit < len(LOAD_UNITS):
-                    load(unit)
+            c0 = i * OW
+            n_v = V_RELU if i % 2 == 1 else 0
+            if n_v:
+                lo = words[:, c0 : c0 + n_v]
+                nc.vector.tensor_scalar_max(out=lo, in0=lo, scalar1=0.0)
+            hi = words[:, c0 + n_v : c0 + OW]
+            nc.scalar.activation(out=hi, in_=hi, func=RELU)
+            if i in store_ending:
+                i0, n = store_ending[i]
+                cols = slice(i0 * OW, (i0 + n) * OW)
+                nc.sync.dma_start(out=out_v[:, cols], in_=words[:, cols])
 
-        transposes(0)
         bias_matmuls()
+        bias_copies()
+        transposes(0)
         w_regroup(0)
         w_regroup(1)
         w_quantise(0)
         w_quantise(1)
         w_regroup(2)
         w_regroup(3)
-        w_quantise(2)
-        w_quantise(3)
         for s in range(NT + 3):
-            if s + 1 < NT:
+            if s + 1 < NT and s >= 4:
                 transposes(s + 1)
             if 0 <= s - 1 < NT:
                 quantise(s - 1)
             if s < NT:
                 copies(s)
-            if s == 0:
-                bias_copies()
+            if s == 1:
+                w_quantise(2)
+                w_quantise(3)
             if 0 <= s - 1 < NT:
                 passes(s - 1)
+            if s + 1 < NT and s < 4:
+                transposes(s + 1)
             if 0 <= s - 2 < NT:
                 adds(s - 2)
             if 0 <= s - 3 < NT:

@@ -19,7 +19,7 @@ NT = ROWS // P
 XW = MASKS * FEAT
 OW = MASKS * UNITS
 PIN = True
-V_RELU = 512
+V_RELU = 768
 
 LOAD_UNITS = [(0, 1), (1, 1), (2, 1), (3, 1), (4, 2), (6, 2), (8, 4), (12, 4), (16, 8), (24, 8)]
 STORE_UNITS = [(0, 8), (8, 8), (16, 4), (20, 4), (24, 2), (26, 2), (28, 1), (29, 1), (30, 1), (31, 1)]

@@ -19,9 +19,9 @@ NT = ROWS // P
 XW = MASKS * FEAT
 OW = MASKS * UNITS
 PIN = True
-V_RELU = 768
+V_RELU = 640
 
-LOAD_UNITS = [(0, 1), (1, 1), (2, 1), (3, 1), (4, 2), (6, 2), (8, 4), (12, 4), (16, 8), (24, 8)]
+LOAD_UNITS = [(0, 1), (1, 1), (2, 2), (4, 2), (6, 2), (8, 4), (12, 8), (20, 12)]
 STORE_UNITS = [(0, 8), (8, 8), (16, 4), (20, 4), (24, 2), (26, 2), (28, 1), (29, 1), (30, 1), (31, 1)]
 
 
@@ -63,10 +63,11 @@ def tile_paralleldense_t_kernel(tc, x, W, b, out):
             )
 
         load_w(0)
-        nc.sync.dma_start(out=brow[0:1, :], in_=b.rearrange("(o m) u -> o (m u)", o=1))
         load(0)
         load_w(2)
-        for unit in range(1, len(LOAD_UNITS)):
+        load(1)
+        nc.sync.dma_start(out=brow[0:1, :], in_=b.rearrange("(o m) u -> o (m u)", o=1))
+        for unit in range(2, len(LOAD_UNITS)):
             load(unit)
 
         bias = const.tile([P, OW], F32, name="bias")
@@ -174,8 +175,6 @@ def tile_paralleldense_t_kernel(tc, x, W, b, out):
                 cols = slice(i0 * OW, (i0 + n) * OW)
                 nc.sync.dma_start(out=out_v[:, cols], in_=words[:, cols])
 
-        bias_matmuls()
-        bias_copies()
         transposes(0)
         w_regroup(0)
         w_regroup(1)
@@ -195,6 +194,9 @@ def tile_paralleldense_t_kernel(tc, x, W, b, out):
                 w_quantise(3)
             if 0 <= s - 1 < NT:
                 passes(s - 1)
+            if s == 1:
+                bias_matmuls()
+                bias_copies()
             if s + 1 < NT and s < 4:
                 transposes(s + 1)
             if 0 <= s - 2 < NT:

@@ -19,7 +19,7 @@ NT = ROWS // P
 XW = MASKS * FEAT
 OW = MASKS * UNITS
 PIN = True
-V_RELU = 640
+V_RELU = 288
 
 LOAD_UNITS = [(0, 1), (1, 1), (2, 2), (4, 2), (6, 2), (8, 4), (12, 8), (20, 12)]
 STORE_UNITS = [(0, 8), (8, 8), (16, 4), (20, 4), (24, 2), (26, 2), (28, 1), (29, 1), (30, 1), (31, 1)]
@@ -164,11 +164,9 @@ def tile_paralleldense_t_kernel(tc, x, W, b, out):
 
         def relu_store(i):
             c0 = i * OW
-            n_v = V_RELU if i % 2 == 1 else 0
-            if n_v:
-                lo = words[:, c0 : c0 + n_v]
-                nc.vector.tensor_scalar_max(out=lo, in0=lo, scalar1=0.0)
-            hi = words[:, c0 + n_v : c0 + OW]
+            lo = words[:, c0 : c0 + V_RELU]
+            nc.vector.tensor_scalar_max(out=lo, in0=lo, scalar1=0.0)
+            hi = words[:, c0 + V_RELU : c0 + OW]
             nc.scalar.activation(out=hi, in_=hi, func=RELU)
             if i in store_ending:
                 i0, n = store_ending[i]

@@ -20,9 +20,10 @@ XW = MASKS * FEAT
 OW = MASKS * UNITS
 PIN = True
 V_RELU = 288
+DRAIN = 29
 
 LOAD_UNITS = [(0, 1), (1, 1), (2, 2), (4, 2), (6, 2), (8, 4), (12, 8), (20, 12)]
-STORE_UNITS = [(0, 8), (8, 8), (16, 4), (20, 4), (24, 2), (26, 2), (28, 1), (29, 1), (30, 1), (31, 1)]
+STORE_UNITS = [(0, 8), (8, 8), (16, 4), (20, 4), (24, 2), (26, 2), (28, 1), (29, 1), (30, 1)]
 
 
 def tile_paralleldense_t_kernel(tc, x, W, b, out):
@@ -63,10 +64,10 @@ def tile_paralleldense_t_kernel(tc, x, W, b, out):
             )
 
         load_w(0)
+        nc.sync.dma_start(out=brow[0:1, :], in_=b.rearrange("(o m) u -> o (m u)", o=1))
         load(0)
         load_w(2)
         load(1)
-        nc.sync.dma_start(out=brow[0:1, :], in_=b.rearrange("(o m) u -> o (m u)", o=1))
         for unit in range(2, len(LOAD_UNITS)):
             load(unit)
 
@@ -152,27 +153,43 @@ def tile_paralleldense_t_kernel(tc, x, W, b, out):
 
         store_ending = {i0 + n - 1: (i0, n) for i0, n in STORE_UNITS}
 
-        def adds(i):
-            c0 = i * OW
-            for h in range(2):
-                nc.vector.tensor_tensor(
-                    out=words[:, c0 + 512 * h : c0 + 512 * h + 512],
-                    in0=acc_of[i][h][:],
-                    in1=bias[:, 512 * h : 512 * h + 512],
-                    op=ADD,
-                )
+        def half(i, h):
+            return words[:, i * OW + 512 * h : i * OW + 512 * h + 512]
+
+        def add_half(i, h):
+            nc.vector.tensor_tensor(
+                out=half(i, h),
+                in0=acc_of[i][h][:],
+                in1=bias[:, 512 * h : 512 * h + 512],
+                op=ADD,
+            )
+
+        def store_half(i, h):
+            nc.sync.dma_start(out=out_v[:, i * OW + 512 * h : i * OW + 512 * h + 512], in_=half(i, h))
+
+        def finish_last(i):
+            add_half(i, 0)
+            nc.scalar.activation(out=half(i, 0), in_=half(i, 0), func=RELU)
+            store_half(i, 0)
+            add_half(i, 1)
+            nc.vector.tensor_scalar_max(out=half(i, 1), in0=half(i, 1), scalar1=0.0)
+            store_half(i, 1)
 
         def relu_store(i):
             c0 = i * OW
-            lo = words[:, c0 : c0 + V_RELU]
-            nc.vector.tensor_scalar_max(out=lo, in0=lo, scalar1=0.0)
-            hi = words[:, c0 + V_RELU : c0 + OW]
+            v_cols = V_RELU if i < DRAIN else 0
+            if v_cols > 0:
+                lo = words[:, c0 : c0 + v_cols]
+                nc.vector.tensor_scalar_max(out=lo, in0=lo, scalar1=0.0)
+            hi = words[:, c0 + v_cols : c0 + OW]
             nc.scalar.activation(out=hi, in_=hi, func=RELU)
             if i in store_ending:
                 i0, n = store_ending[i]
                 cols = slice(i0 * OW, (i0 + n) * OW)
                 nc.sync.dma_start(out=out_v[:, cols], in_=words[:, cols])
 
+        bias_matmuls()
+        bias_copies()
         transposes(0)
         w_regroup(0)
         w_regroup(1)
@@ -180,7 +197,7 @@ def tile_paralleldense_t_kernel(tc, x, W, b, out):
         w_quantise(1)
         w_regroup(2)
         w_regroup(3)
-        for s in range(NT + 3):
+        for s in range(NT + 1):
             if s + 1 < NT and s >= 4:
                 transposes(s + 1)
             if 0 <= s - 1 < NT:
@@ -192,12 +209,12 @@ def tile_paralleldense_t_kernel(tc, x, W, b, out):
                 w_quantise(3)
             if 0 <= s - 1 < NT:
                 passes(s - 1)
-            if s == 1:
-                bias_matmuls()
-                bias_copies()
             if s + 1 < NT and s < 4:
                 transposes(s + 1)
-            if 0 <= s - 2 < NT:
-                adds(s - 2)
-            if 0 <= s - 3 < NT:
+            if s >= 2:
+                add_half(s - 2, 0)
+                add_half(s - 2, 1)
+            if s >= 3:
                 relu_store(s - 3)
+        relu_store(NT - 2)
+        finish_last(NT - 1)

from contextlib import ExitStack

import concourse.mybir as mybir
from concourse.masks import make_identity

F32 = mybir.dt.float32
BF16 = mybir.dt.bfloat16
U32 = mybir.dt.uint32
U8 = mybir.dt.uint8
FP8X4 = mybir.dt.float8_e4m3fn_x4
ADD = mybir.AluOpType.add
RELU = mybir.ActivationFunctionType.Relu

P = 128
ROWS, MASKS, FEAT, UNITS = 4096, 4, 512, 256
FLOPS = 2 * ROWS * MASKS * FEAT * UNITS

NT = ROWS // P
XW = MASKS * FEAT
OW = MASKS * UNITS
PIN = True
V_RELU = 288
DRAIN = 29

LOAD_UNITS = [(0, 1), (1, 1), (2, 2), (4, 2), (6, 2), (8, 4), (12, 8), (20, 12)]
STORE_UNITS = [(0, 8), (8, 8), (16, 4), (20, 4), (24, 2), (26, 2), (28, 1), (29, 1), (30, 1)]


def tile_paralleldense_t_kernel(tc, x, W, b, out):
    nc = tc.nc
    x_v = x.rearrange("(p t) m f -> p (t m f)", p=P, t=NT)
    out_v = out.rearrange("(p t) n -> p (t n)", p=P, t=NT)
    w_v = W.rearrange("m (q t) c -> q m (t c)", q=P, t=4)

    with ExitStack() as ctx:
        if PIN:
            ctx.enter_context(tc.manual_schedule())
        const = ctx.enter_context(tc.tile_pool(name="const", bufs=1))
        gpool = ctx.enter_context(tc.tile_pool(name="gpool", bufs=3))
        qpool = ctx.enter_context(tc.tile_pool(name="qpool", bufs=3))
        tpool = ctx.enter_context(tc.psum_pool(name="tpool", bufs=4))
        apool = ctx.enter_context(tc.psum_pool(name="apool", bufs=4))

        xo = const.tile([P, NT * XW], BF16, name="xo")
        words = xo[:].bitcast(F32)

        def load(unit):
            i0, n = LOAD_UNITS[unit]
            cols = slice(i0 * XW, (i0 + n) * XW)
            nc.sync.dma_start(out=xo[:, cols], in_=x_v[:, cols])

        brow = const.tile([P, OW], BF16, name="brow")
        nc.vector.memset(brow[:].bitcast(U32), 0)
        ones = const.tile([P, P], BF16, name="ones")
        nc.vector.memset(ones[:], 1.0)
        ident = const.tile([P, P], F32, name="ident")
        make_identity(nc, ident[:])
        w_raw = const.tile([P, MASKS, 4, UNITS], BF16, name="w_raw")

        def load_w(m0):
            nc.sync.dma_start(
                out=w_raw[:, m0 : m0 + 2].rearrange("q m t c -> q m (t c)"),
                in_=w_v[:, m0 : m0 + 2],
            )

        load_w(0)
        nc.sync.dma_start(out=brow[0:1, :], in_=b.rearrange("(o m) u -> o (m u)", o=1))
        load(0)
        load_w(2)
        load(1)
        for unit in range(2, len(LOAD_UNITS)):
            load(unit)

        bias = const.tile([P, OW], F32, name="bias")
        bias_banks = []

        def bias_matmuls():
            for h in range(2):
                bp = apool.tile([P, 512], F32, name="acc")
                nc.tensor.matmul(out=bp[:], lhsT=ones[:], rhs=brow[:, 512 * h : 512 * h + 512], start=True, stop=True)
                bias_banks.append(bp)

        def bias_copies():
            for h in range(2):
                nc.scalar.copy(out=bias[:, 512 * h : 512 * h + 512], in_=bias_banks[h][:])

        w_grp = const.tile([P, MASKS, UNITS, 4], BF16, name="w_grp", align_bytes=64)
        w_codes = const.tile([P, MASKS * UNITS], U32, name="w_codes", align_bytes=64)
        w_scales = const.tile([P, MASKS * UNITS], U8, name="w_scales", align_bytes=64)

        def w_regroup(m):
            nc.vector.tensor_copy(
                out=w_grp[:, m].rearrange("q (c i) t -> q c t i", i=4),
                in_=w_raw[:, m].rearrange("q t (c i) -> q c t i", i=4),
            )

        def w_quantise(m):
            cols = slice(UNITS * m, UNITS * m + UNITS)
            nc.vector.quantize_mx(
                out=w_codes[:, cols].bitcast(FP8X4),
                scales=w_scales[:, cols],
                in_=w_grp[:, m].rearrange("q c t -> q (c t)"),
            )

        tp_of, grp_of, q_of, acc_of = {}, {}, {}, {}

        def transposes(i):
            c0 = i * OW
            banks = []
            for h in range(2):
                tpb = tpool.tile([P, 512], F32, name="tpb")
                for j in range(4):
                    ml, u = divmod(j, 2)
                    col = c0 + 256 * (2 * h + ml) + u
                    nc.tensor.transpose(tpb[:, P * j : P * j + P], words[:, col : col + 255 : 2], ident[:])
                banks.append(tpb)
            tp_of[i] = banks

        def copies(i):
            grp = gpool.tile([P, 4 * MASKS * P], BF16, name="grp", align_bytes=64)
            gw = grp[:].bitcast(F32)
            for h in range(2):
                nc.scalar.copy(
                    out=gw[:, 512 * h : 512 * h + 512].rearrange("q (m i u) -> q m i u", m=2, u=2),
                    in_=tp_of[i][h][:].rearrange("q (m u i) -> q m i u", m=2, u=2),
                )
            grp_of[i] = grp

        def quantise(i):
            codes = qpool.tile([P, MASKS * P], U32, name="codes", align_bytes=64)
            scales = qpool.tile([P, MASKS * P], U8, name="scales", align_bytes=64)
            nc.vector.quantize_mx(out=codes[:].bitcast(FP8X4), scales=scales[:], in_=grp_of[i][:])
            q_of[i] = (codes, scales)

        def passes(i):
            codes, scales = q_of[i]
            banks = []
            for h in range(2):
                acc = apool.tile([P, 512], F32, name="acc")
                for ml in range(2):
                    m = 2 * h + ml
                    nc.tensor.matmul_mx(
                        out=acc[:, UNITS * ml : UNITS * ml + UNITS],
                        lhsT=codes[:, P * m : P * m + P].bitcast(FP8X4),
                        lhsT_scale=scales[:, P * m : P * m + P],
                        rhs=w_codes[:, UNITS * m : UNITS * m + UNITS].bitcast(FP8X4),
                        rhs_scale=w_scales[:, UNITS * m : UNITS * m + UNITS],
                        start=True,
                        stop=True,
                    )
                banks.append(acc)
            acc_of[i] = banks

        store_ending = {i0 + n - 1: (i0, n) for i0, n in STORE_UNITS}

        def half(i, h):
            return words[:, i * OW + 512 * h : i * OW + 512 * h + 512]

        def add_half(i, h):
            nc.vector.tensor_tensor(
                out=half(i, h),
                in0=acc_of[i][h][:],
                in1=bias[:, 512 * h : 512 * h + 512],
                op=ADD,
            )

        def store_half(i, h):
            nc.sync.dma_start(out=out_v[:, i * OW + 512 * h : i * OW + 512 * h + 512], in_=half(i, h))

        def finish_last(i):
            add_half(i, 0)
            nc.scalar.activation(out=half(i, 0), in_=half(i, 0), func=RELU)
            store_half(i, 0)
            add_half(i, 1)
            nc.vector.tensor_scalar_max(out=half(i, 1), in0=half(i, 1), scalar1=0.0)
            store_half(i, 1)

        def relu_store(i):
            c0 = i * OW
            v_cols = V_RELU if i < DRAIN else 0
            if v_cols > 0:
                lo = words[:, c0 : c0 + v_cols]
                nc.vector.tensor_scalar_max(out=lo, in0=lo, scalar1=0.0)
            hi = words[:, c0 + v_cols : c0 + OW]
            nc.scalar.activation(out=hi, in_=hi, func=RELU)
            if i in store_ending:
                i0, n = store_ending[i]
                cols = slice(i0 * OW, (i0 + n) * OW)
                nc.sync.dma_start(out=out_v[:, cols], in_=words[:, cols])

        bias_matmuls()
        bias_copies()
        transposes(0)
        w_regroup(0)
        w_regroup(1)
        w_quantise(0)
        w_quantise(1)
        w_regroup(2)
        w_regroup(3)
        for s in range(NT + 1):
            if s + 1 < NT and s >= 4:
                transposes(s + 1)
            if 0 <= s - 1 < NT:
                quantise(s - 1)
            if s < NT:
                copies(s)
            if s == 1:
                w_quantise(2)
                w_quantise(3)
            if 0 <= s - 1 < NT:
                passes(s - 1)
            if s + 1 < NT and s < 4:
                transposes(s + 1)
            if s >= 2:
                add_half(s - 2, 0)
                add_half(s - 2, 1)
            if s >= 3:
                relu_store(s - 3)
        relu_store(NT - 2)
        finish_last(NT - 1)
